import numpy as np
import ml_dtypes

BF16 = ml_dtypes.bfloat16


def bf(x):
    return np.asarray(x, np.float32).astype(BF16)


def f32(x):
    return np.asarray(x, np.float32)


def f64(x):
    return np.asarray(x).astype(np.float64)


def striped(idx):
    return np.tile(idx.reshape(-1, 16).T, (8, 1))


T, K, S, N = 512, 512, 512, 256
ALPHA = 0.75


def setup_inputs():
    return {"base": f32(np.random.standard_normal((T, S))), "x": bf(np.random.standard_normal((K, T))), "w": bf(np.random.standard_normal((K, N)) / np.sqrt(K)), "scale": f32(1.0 + 0.1 * np.random.standard_normal((1, N))), "bias": f32(0.1 * np.random.standard_normal((1, N))), "offs": striped(np.random.permutation(S)[:N])}


def reference(base, x, w, scale, bias, offs):
    idx = offs[:16].T.reshape(-1)
    y = f64(x).T @ f64(w)
    out = f64(base).copy()
    out[:, idx] = y * (ALPHA * f64(scale)) + f64(bias)
    return out

@@ -1,0 +1,94 @@
+import concourse.mybir as mybir
+
+P = 128
+QUAD = 32
+T, K, S, N = 512, 512, 512, 256
+ALPHA = 0.75
+T_BLOCKS = T // P
+K_BLOCKS = K // P
+FLOPS = 2 * T * K * N
+
+BF16, F32, U16 = mybir.dt.bfloat16, mybir.dt.float32, mybir.dt.uint16
+MULT, ADD = mybir.AluOpType.mult, mybir.AluOpType.add
+
+
+def by_blocks(tile):
+    return tile[:].rearrange("p (b k) -> p b k", k=QUAD)
+
+
+def tile_tuckerlinear_kernel(tc, base, x, w, scale, bias, offs, out):
+    nc = tc.nc
+    with (
+        tc.tile_pool(name="held", bufs=1) as held,
+        tc.tile_pool(name="blocks", bufs=T_BLOCKS) as blocks,
+        tc.psum_pool(name="psum", bufs=T_BLOCKS) as psum,
+    ):
+        names = ("gain", "bias")
+        factors = (ALPHA, 1.0)
+        seeded = [held.tile([P, N], F32, name=f"{name}_seeded", align_bytes=64) for name in names]
+        for tile, engine in zip(seeded, (nc.vector, nc.gpsimd)):
+            engine.memset(tile[:], 0.0)
+
+        offsets = held.tile([P, N // 16], U16, name="offsets")
+        w_sb = held.tile([P, K_BLOCKS, N], BF16, name="w_sb")
+        w_by_blocks = w.rearrange("(p kb) n -> p kb n", kb=K_BLOCKS)
+
+        x_blocks = [blocks.tile([P, K_BLOCKS, P], BF16, name="x_block") for tb in range(T_BLOCKS)]
+        windows = [blocks.tile([P, S], F32, name="window") for tb in range(T_BLOCKS)]
+
+        def load_x(tb):
+            tokens = slice(tb * P, (tb + 1) * P)
+            nc.sync.dma_start(x_blocks[tb][:], x[:, tokens].rearrange("(p kb) t -> p kb t", kb=K_BLOCKS))
+
+        def load_window(tb):
+            nc.sync.dma_start(windows[tb][:], base[tb * P : (tb + 1) * P, :])
+
+        def load_row(tile, row, queue):
+            first_partitions = tile[:].rearrange("(q i) n -> q i n", i=QUAD)[:, 0, :]
+            queue.dma_start(first_partitions, row.to_broadcast([P // QUAD, N]))
+
+        load_x(0)
+        load_row(seeded[0], scale, nc.scalar)
+        load_row(seeded[1], bias, nc.sync)
+        for half in (slice(0, K_BLOCKS // 2), slice(K_BLOCKS // 2, K_BLOCKS)):
+            nc.sync.dma_start(w_sb[:, half, :], w_by_blocks[:, half, :])
+        nc.sync.dma_start(offsets[:], offs)
+        load_window(0)
+        for tb in range(1, T_BLOCKS):
+            load_x(tb)
+        for tb in range(1, T_BLOCKS):
+            load_window(tb)
+
+        turned = [held.tile([P, N], F32, name=f"{name}_turned", align_bytes=64) for name in names]
+        for r in range(len(names)):
+            nc.vector.transpose(turned[r][:], seeded[r][:])
+        widened = [held.tile([P, N], F32, name=f"{name}_widened", align_bytes=64) for name in names]
+        for r in range(len(names)):
+            column0 = by_blocks(turned[r])[:, :, 0:1].to_broadcast([P, N // QUAD, QUAD])
+            nc.vector.tensor_scalar_mul(by_blocks(widened[r]), column0, factors[r])
+        spread = [held.tile([P, N], F32, name=f"{name}_all", align_bytes=64) for name in names]
+        for r in range(len(names)):
+            nc.vector.transpose(spread[r][:], widened[r][:])
+        gain_all, bias_all = spread
+
+        def scaled_product(tb):
+            product = psum.tile([P, N], F32, name="product")
+            for kb in range(K_BLOCKS):
+                nc.tensor.matmul(
+                    product[:],
+                    x_blocks[tb][:, kb, :],
+                    w_sb[:, kb, :],
+                    start=(kb == 0),
+                    stop=(kb == K_BLOCKS - 1),
+                )
+            scaled = blocks.tile([P, N], F32, name="scaled")
+            nc.vector.tensor_tensor(scaled[:], product[:], gain_all[:], MULT)
+            return scaled
+
+        scaled_next = scaled_product(0)
+        for tb in range(T_BLOCKS):
+            scaled = scaled_next
+            if tb + 1 < T_BLOCKS:
+                scaled_next = scaled_product(tb + 1)
+            nc.vector.tensor_tensor(windows[tb][:].indirect(offsets[:]), scaled[:], bias_all[:], ADD)
+            nc.scalar.dma_start(out[tb * P : (tb + 1) * P, :], windows[tb][:])

@@ -25,7 +25,7 @@ def tile_tuckerlinear_kernel(tc, base, x, w, scale, bias, offs, out):
     ):
         names = ("gain", "bias")
         factors = (ALPHA, 1.0)
-        seeded = [held.tile([P, N], F32, name=f"{name}_seeded", align_bytes=64) for name in names]
+        seeded = [held.tile([P, N + 1], F32, name=f"{name}_seeded", align_bytes=64) for name in names]
         for tile, engine in zip(seeded, (nc.vector, nc.gpsimd)):
             engine.memset(tile[:], 0.0)
 
@@ -44,7 +44,7 @@ def tile_tuckerlinear_kernel(tc, base, x, w, scale, bias, offs, out):
             nc.sync.dma_start(windows[tb][:], base[tb * P : (tb + 1) * P, :])
 
         def load_row(tile, row, queue):
-            first_partitions = tile[:].rearrange("(q i) n -> q i n", i=QUAD)[:, 0, :]
+            first_partitions = tile[:, :N].rearrange("(q i) n -> q i n", i=QUAD)[:, 0, :]
             queue.dma_start(first_partitions, row.to_broadcast([P // QUAD, N]))
 
         load_x(0)
@@ -61,7 +61,7 @@ def tile_tuckerlinear_kernel(tc, base, x, w, scale, bias, offs, out):
 
         turned = [held.tile([P, N], F32, name=f"{name}_turned", align_bytes=64) for name in names]
         for r in range(len(names)):
-            nc.vector.transpose(turned[r][:], seeded[r][:])
+            nc.vector.transpose(turned[r][:], seeded[r][:, :N])
         widened = [held.tile([P, N], F32, name=f"{name}_widened", align_bytes=64) for name in names]
         for r in range(len(names)):
             column0 = by_blocks(turned[r])[:, :, 0:1].to_broadcast([P, N // QUAD, QUAD])

import concourse.mybir as mybir

P = 128
QUAD = 32
T, K, S, N = 512, 512, 512, 256
ALPHA = 0.75
T_BLOCKS = T // P
K_BLOCKS = K // P
FLOPS = 2 * T * K * N

BF16, F32, U16 = mybir.dt.bfloat16, mybir.dt.float32, mybir.dt.uint16
MULT, ADD = mybir.AluOpType.mult, mybir.AluOpType.add


def by_blocks(tile):
    return tile[:].rearrange("p (b k) -> p b k", k=QUAD)


def tile_tuckerlinear_kernel(tc, base, x, w, scale, bias, offs, out):
    nc = tc.nc
    with (
        tc.tile_pool(name="held", bufs=1) as held,
        tc.tile_pool(name="blocks", bufs=T_BLOCKS) as blocks,
        tc.psum_pool(name="psum", bufs=T_BLOCKS) as psum,
    ):
        names = ("gain", "bias")
        factors = (ALPHA, 1.0)
        seeded = [held.tile([P, N + 1], F32, name=f"{name}_seeded", align_bytes=64) for name in names]
        for tile, engine in zip(seeded, (nc.vector, nc.gpsimd)):
            engine.memset(tile[:], 0.0)

        offsets = held.tile([P, N // 16], U16, name="offsets")
        w_sb = held.tile([P, K_BLOCKS, N], BF16, name="w_sb")
        w_by_blocks = w.rearrange("(p kb) n -> p kb n", kb=K_BLOCKS)

        x_blocks = [blocks.tile([P, K_BLOCKS, P], BF16, name="x_block") for tb in range(T_BLOCKS)]
        windows = [blocks.tile([P, S], F32, name="window") for tb in range(T_BLOCKS)]

        def load_x(tb):
            tokens = slice(tb * P, (tb + 1) * P)
            nc.sync.dma_start(x_blocks[tb][:], x[:, tokens].rearrange("(p kb) t -> p kb t", kb=K_BLOCKS))

        def load_window(tb):
            nc.sync.dma_start(windows[tb][:], base[tb * P : (tb + 1) * P, :])

        def load_row(tile, row, queue):
            first_partitions = tile[:, :N].rearrange("(q i) n -> q i n", i=QUAD)[:, 0, :]
            queue.dma_start(first_partitions, row.to_broadcast([P // QUAD, N]))

        load_x(0)
        load_row(seeded[0], scale, nc.scalar)
        load_row(seeded[1], bias, nc.sync)
        for half in (slice(0, K_BLOCKS // 2), slice(K_BLOCKS // 2, K_BLOCKS)):
            nc.sync.dma_start(w_sb[:, half, :], w_by_blocks[:, half, :])
        nc.sync.dma_start(offsets[:], offs)
        load_window(0)
        for tb in range(1, T_BLOCKS):
            load_x(tb)
        for tb in range(1, T_BLOCKS):
            load_window(tb)

        turned = [held.tile([P, N], F32, name=f"{name}_turned", align_bytes=64) for name in names]
        for r in range(len(names)):
            nc.vector.transpose(turned[r][:], seeded[r][:, :N])
        widened = [held.tile([P, N], F32, name=f"{name}_widened", align_bytes=64) for name in names]
        for r in range(len(names)):
            column0 = by_blocks(turned[r])[:, :, 0:1].to_broadcast([P, N // QUAD, QUAD])
            nc.vector.tensor_scalar_mul(by_blocks(widened[r]), column0, factors[r])
        spread = [held.tile([P, N], F32, name=f"{name}_all", align_bytes=64) for name in names]
        for r in range(len(names)):
            nc.vector.transpose(spread[r][:], widened[r][:])
        gain_all, bias_all = spread

        def scaled_product(tb):
            product = psum.tile([P, N], F32, name="product")
            for kb in range(K_BLOCKS):
                nc.tensor.matmul(
                    product[:],
                    x_blocks[tb][:, kb, :],
                    w_sb[:, kb, :],
                    start=(kb == 0),
                    stop=(kb == K_BLOCKS - 1),
                )
            scaled = blocks.tile([P, N], F32, name="scaled")
            nc.vector.tensor_tensor(scaled[:], product[:], gain_all[:], MULT)
            return scaled

        scaled_next = scaled_product(0)
        for tb in range(T_BLOCKS):
            scaled = scaled_next
            if tb + 1 < T_BLOCKS:
                scaled_next = scaled_product(tb + 1)
            nc.vector.tensor_tensor(windows[tb][:].indirect(offsets[:]), scaled[:], bias_all[:], ADD)
            nc.scalar.dma_start(out[tb * P : (tb + 1) * P, :], windows[tb][:])
